import numpy as np
import ml_dtypes


def mxq(x, axis, fmt="e4m3"):
    dtype, down = {"e4m3": (ml_dtypes.float8_e4m3fn, 7), "e5m2": (ml_dtypes.float8_e5m2, 14)}[fmt]
    v = np.moveaxis(np.asarray(x, np.float32).astype(ml_dtypes.bfloat16).astype(np.float64), axis, -1)
    blocks = v.reshape(v.shape[:-1] + (-1, 32))
    amax = np.abs(blocks).max(-1, keepdims=True)
    byte = np.maximum(np.where(amax > 0, np.frexp(amax)[1] - 1 + 127, 0) - down, 1)
    scale = np.exp2(byte - 127.0)
    codes = (blocks / scale).astype(np.float32).astype(dtype).astype(np.float64)
    return np.moveaxis((codes * scale).reshape(v.shape), -1, axis)


WIDE = False


def mx_kscale(k):
    if not WIDE:
        return np.ones(k)
    levels = np.array([10, -10, 5, -5, 0])
    if k % 512:
        return np.exp2(np.random.permutation(np.resize(levels, k // 32))).repeat(32)
    a = np.empty((k // 512, 16))
    for p in range(k // 512):
        a[p, :8] = np.random.permutation(np.resize(levels, 8))
        for g in range(8):
            far = levels[np.abs(levels - a[p, g]) >= 10]
            a[p, g + 8] = far[np.random.randint(len(far))]
    return np.exp2(a.ravel()).repeat(32)


BF16 = ml_dtypes.bfloat16


def bf(x):
    return np.asarray(x, np.float32).astype(BF16)


def f64(x):
    return np.asarray(x).astype(np.float64)


B, T, D, DEPTH, F = 4, 1024, 1024, 4, 32
L = 2 ** DEPTH
N = L - 1
LF = L * F


def sigmoid(v):
    return 1.0 / (1.0 + np.exp(-v))


def leaf_probs(c):
    probs = np.ones(c.shape[:-1] + (1,))
    for m in range(DEPTH):
        start = 2 ** m - 1
        cl = c[..., start:start + 2 ** m]
        probs = np.stack([probs * cl, probs * (1.0 - cl)], axis=-1)
        probs = probs.reshape(probs.shape[:-2] + (-1,))
    return probs


def draw0():
    s = mx_kscale(D)
    t = mx_kscale(LF).reshape(L, F)
    return {"x": bf(np.random.standard_normal((B, T, D)) * s),
            "node_logits": bf(np.random.standard_normal((B, T, N)) * 1.5),
            "node_b": bf(np.random.standard_normal(N) * 0.5),
            "w1": bf(np.random.standard_normal((L, D, F)) / np.sqrt(D) / s[None, :, None] * t[:, None, :]),
            "b1": bf(np.random.standard_normal((L, F)) * 0.5 * t),
            "w2": bf(np.random.standard_normal((L, F, D)) * 2.0 / np.sqrt(F) / t[:, :, None])}


def core(x, node_logits, node_b, w1, b1, w2):
    probs = leaf_probs(sigmoid(f64(node_logits) + f64(node_b)))
    w1f = f64(w1).transpose(1, 0, 2).reshape(D, LF)
    a = mxq(f64(x), 2, "e4m3") @ mxq(w1f, 0, "e4m3")
    h = np.maximum(a.reshape(B, T, L, F) + f64(b1), 0.0) * probs[..., None]
    return mxq(h.reshape(B, T, LF), 2, "e4m3") @ mxq(f64(w2).reshape(LF, D), 0, "e4m3")


def e4m3fn_bytes(y):
    return np.clip(np.asarray(y, np.float64), -448.0, 448.0).astype(np.float32).astype(ml_dtypes.float8_e4m3fn).view(np.uint8)


def e4m3fn_values(b):
    return np.asarray(b, np.uint8).view(ml_dtypes.float8_e4m3fn).astype(np.float64)


def setup_inputs():
    d = draw0()
    x0 = np.asarray(d['x']).astype(np.float64)
    s = (np.max(np.abs(x0), axis=(0, 1), keepdims=True) / 448.0).astype(np.float32)
    out = {}
    for k, v in d.items():
        if k == 'x':
            out['x_bytes'] = e4m3fn_bytes(x0 / s.astype(np.float64))
            out['x_scale'] = s
        else:
            out[k] = v
    return out


def reference(x_bytes, x_scale, node_logits, node_b, w1, b1, w2):
    return core(e4m3fn_values(x_bytes) * x_scale.astype(np.float64), node_logits, node_b, w1, b1, w2)

from contextlib import ExitStack

import concourse.mybir as mybir
from concourse.masks import make_identity

F32 = mybir.dt.float32
BF16 = mybir.dt.bfloat16
U32 = mybir.dt.uint32
U8 = mybir.dt.uint8
FP8 = mybir.dt.float8_e4m3fn
FP8X4 = mybir.dt.float8_e4m3fn_x4
ACT = mybir.ActivationFunctionType
OP = mybir.AluOpType

P = 128
TOKENS = 4096
D = 1024
LF = 512
E = 1024
LEAVES = 16
NODES = 15
TILES = TOKENS // P
PAIRS = TILES // 2
FLOPS = 2 * TOKENS * D * LF + 2 * TOKENS * LF * E

X_CHUNKS = [(0, 1), (1, 2), (2, 4), (4, 8), (8, 12), (12, 16), (16, 20), (20, 24), (24, 28), (28, 32)]


def tile_fastfeedforwardnetwork_pa_t_kernel(tc, x_bytes, x_scale, node_logits, node_b, w1, b1, w2, out):
    nc = tc.nc
    x_v = x_bytes.rearrange("b s k -> (b s) k").rearrange("(p i) k -> p i k", i=TILES)
    out_v = out.rearrange("b s e -> (b s) e").rearrange("(p i) e -> p i e", i=TILES)
    logits_v = node_logits.rearrange("b s v -> (b s) v").rearrange("(p i) v -> p (i v)", i=TILES)
    scale_v = x_scale.rearrange("a b k -> (a b k)")
    b1_v = b1.rearrange("l f -> (l f)").rearrange("(m t) -> m t", t=4)
    w2_v = w2.rearrange("l f e -> (l f) e").rearrange("(p j) e -> p j e", j=4)

    with ExitStack() as ctx:
        keep = ctx.enter_context(tc.tile_pool(name="keep", bufs=1))
        xs_pool = ctx.enter_context(tc.tile_pool(name="xs", bufs=4))
        xg_pool = ctx.enter_context(tc.tile_pool(name="xg", bufs=2))
        xq_pool = ctx.enter_context(tc.tile_pool(name="xq", bufs=2))
        h_pool = ctx.enter_context(tc.tile_pool(name="h", bufs=2))
        hq_pool = ctx.enter_context(tc.tile_pool(name="hq", bufs=3))
        o_pool = ctx.enter_context(tc.tile_pool(name="o", bufs=4))
        xt_psum = ctx.enter_context(tc.psum_pool(name="xt_psum", bufs=2))
        a_psum = ctx.enter_context(tc.psum_pool(name="a_psum", bufs=2))
        p_psum = ctx.enter_context(tc.psum_pool(name="p_psum", bufs=1))
        o_psum = ctx.enter_context(tc.psum_pool(name="o_psum", bufs=3))
        ctx.enter_context(tc.manual_schedule())

        x8 = {}

        def load_x(a, b):
            t = keep.tile([P, b - a, D], U8, name=f"x8_{a}")
            nc.sync.dma_start(out=t[:], in_=x_v[:, a:b, :])
            for i in range(a, b):
                x8[i] = t[:, i - a, :]

        logits = keep.tile([P, TILES * NODES], BF16, name="logits")
        nc.scalar.dma_start(out=logits[:], in_=logits_v)
        bias_n = keep.tile([P, NODES], BF16, name="bias_n")
        nc.scalar.dma_start(out=bias_n[:], in_=node_b.partition_broadcast(P))
        bias_h = keep.tile([P, 4], BF16, name="bias_h")
        nc.scalar.dma_start(out=bias_h[:], in_=b1_v)

        load_x(0, 1)
        scale = keep.tile([P, D], F32, name="scale")
        nc.sync.dma_start(out=scale[:, 0:512], in_=scale_v[0:512].partition_broadcast(P))
        nc.sync.dma_start(out=scale[:, 512:1024], in_=scale_v[512:1024].partition_broadcast(P))
        w1_raw = keep.tile([P, 2, LEAVES, P], BF16, name="w1_raw")

        def load_w1(g):
            nc.sync.dma_start(
                out=w1_raw[:, g, :, :],
                in_=w1[:, 512 * g : 512 * (g + 1), :].rearrange("l (p j) f -> p l (j f)", j=4),
            )

        load_w1(0)
        load_x(1, 2)
        load_x(2, 4)
        load_w1(1)
        load_x(4, 8)
        w2_raw = keep.tile([P, 4, E], BF16, name="w2_raw")
        nc.sync.dma_start(out=w2_raw[:], in_=w2_v)
        for a, b in X_CHUNKS[4:]:
            load_x(a, b)

        warm = keep.tile([P, 1], F32, name="warm")
        nc.gpsimd.memset(warm[:], 0.0)
        nc.scalar.activation(out=warm[:], in_=warm[:], func=ACT.Sigmoid)
        ident = keep.tile([P, P], F32, name="ident")
        make_identity(nc, ident[:])

        z = keep.tile([P, TILES, NODES], F32, name="z")
        nc.gpsimd.tensor_tensor(
            out=z[:],
            in0=logits[:].rearrange("p (i v) -> p i v", v=NODES),
            in1=bias_n[:].unsqueeze(1).to_broadcast([P, TILES, NODES]),
            op=OP.add,
        )
        gate = keep.tile([P, 2, TILES, NODES], F32, name="gate")
        nc.scalar.activation(out=gate[:, 0, :, :], in_=z[:], func=ACT.Sigmoid)
        nc.scalar.activation(out=gate[:, 1, :, :], in_=z[:], func=ACT.Sigmoid, scale=-1.0)
        prob = gate[:, :, :, 0].rearrange("p s i -> p i s")
        for level in range(1, 4):
            n = 2**level
            nxt = keep.tile([P, TILES, n, 2], F32, name=f"prob{level}")
            nc.gpsimd.tensor_tensor(
                out=nxt[:],
                in0=prob.unsqueeze(3).to_broadcast([P, TILES, n, 2]),
                in1=gate[:, :, :, n - 1 : 2 * n - 1].rearrange("p s i a -> p i a s"),
                op=OP.mult,
            )
            prob = nxt[:].rearrange("p i a s -> p i (a s)")
        leaf = prob

        w1_g = keep.tile([P, 2, LF, 4], BF16, name="w1_g", align_bytes=64)
        w1_c = keep.tile([P, 2, LF], U32, name="w1_c", align_bytes=64)
        w1_s = keep.tile([P, 2, LF], U8, name="w1_s", align_bytes=64)
        w2_g = keep.tile([P, E, 4], BF16, name="w2_g", align_bytes=64)
        w2_c = keep.tile([P, E], U32, name="w2_c", align_bytes=64)
        w2_s = keep.tile([P, E], U8, name="w2_s", align_bytes=64)

        def w1_interleave(copy, g, t):
            copy(
                out=w1_g[:, g, P * t : P * (t + 1), :].rearrange("p (l h) j -> p l h j", h=8),
                in_=w1_raw[:, g, :, :].rearrange("p l (j h t) -> p l h j t", h=8, t=4)[:, :, :, :, t],
            )

        def w1_quantize(g):
            nc.vector.quantize_mx(
                out=w1_c[:, g, :].bitcast(FP8X4),
                scales=w1_s[:, g, :],
                in_=w1_g[:, g, :, :].rearrange("p n j -> p (n j)"),
            )

        def w2_interleave(copy, a, b):
            copy(
                out=w2_g[:, a:b, :].rearrange("p (c i) j -> p c j i", i=4),
                in_=w2_raw[:, :, a:b].rearrange("p j (c i) -> p c j i", i=4),
            )

        def w2_quantize(a, b):
            nc.vector.quantize_mx(
                out=w2_c[:, a:b].bitcast(FP8X4),
                scales=w2_s[:, a:b],
                in_=w2_g[:, a:b, :].rearrange("p e j -> p (e j)"),
            )

        xs, xt, xg, xq, hp, pt, a_bank, h1, hg, hq, o_bank, o_sb, prep = ({} for unused in range(13))

        def widen(i, parts=1):
            xs[i] = xs_pool.tile([P, D], BF16, name="xs")
            w = D // parts
            for c in range(parts):
                cols = slice(c * w, (c + 1) * w)
                nc.vector.tensor_tensor(
                    out=xs[i][:, cols], in0=x8[i][:, cols].bitcast(FP8), in1=scale[:, cols], op=OP.mult
                )

        def turn_x(i):
            xt[i] = xt_psum.tile([P, 2, 2, P], F32, name="xt")
            words = xs[i][:].bitcast(F32)
            for g in range(2):
                for u in range(2):
                    nc.tensor.transpose(
                        xt[i][:, g, u, :], words[:, 256 * g + u : 256 * (g + 1) : 2], ident[:]
                    )

        def leave_x(i):
            m, j = i // 2, i % 2
            if j == 0:
                xg[m] = xg_pool.tile([P, 2, 256, 4], BF16, name="xg", align_bytes=64)
            words = xg[m][:].rearrange("p g n t -> p g (n t)").bitcast(F32)
            nc.scalar.copy(
                out=words[:, :, 256 * j : 256 * (j + 1)].rearrange("p g (n u) -> p g n u", u=2),
                in_=xt[i][:].rearrange("p g u n -> p g n u"),
            )

        def quant_x(m):
            xq[m] = (
                xq_pool.tile([P, 512], U32, name="xq_c", align_bytes=64),
                xq_pool.tile([P, 512], U8, name="xq_s", align_bytes=64),
            )
            nc.vector.quantize_mx(
                out=xq[m][0][:].bitcast(FP8X4),
                scales=xq[m][1][:],
                in_=xg[m][:].rearrange("p g n t -> p (g n t)"),
            )

        def mm1(m, half):
            a_bank[m, half] = a_psum.tile([P, 2, 256], F32, name="a")
            for s in range(2):
                t = 2 * half + s
                for g in range(2):
                    nc.tensor.matmul_mx(
                        out=a_bank[m, half][:, s, :],
                        lhsT=w1_c[:, g, P * t : P * (t + 1)].bitcast(FP8X4),
                        lhsT_scale=w1_s[:, g, P * t : P * (t + 1)],
                        rhs=xq[m][0][:, 256 * g : 256 * (g + 1)].bitcast(FP8X4),
                        rhs_scale=xq[m][1][:, 256 * g : 256 * (g + 1)],
                        start=(g == 0),
                        stop=(g == 1),
                    )

        def leave_h(m, half):
            if half == 0:
                h1[m] = h_pool.tile([P, 64, 4, 4], F32, name="h1", align_bytes=64)
            for s in range(2):
                t = 2 * half + s
                nc.scalar.activation(
                    out=h1[m][:, :, t, :],
                    in_=a_bank[m, half][:, s, :].rearrange("p (c i) -> p c i", i=4),
                    func=ACT.Relu,
                    bias=bias_h[:, t : t + 1],
                )

        def spread_p(g4):
            prep[g4] = h_pool.tile([P, 512], F32, name="prep")
            nc.vector.tensor_copy(
                out=prep[g4][:].rearrange("p (c r) -> p c r", r=8),
                in_=leaf[:, 4 * g4 : 4 * (g4 + 1), :]
                .rearrange("p i l -> p (i l)")
                .unsqueeze(2)
                .to_broadcast([P, 64, 8]),
            )

        def turn_p(m):
            pt[m] = p_psum.tile([P, 256], F32, name="pt")
            for j in range(2):
                c = 2 * (m % 2) + j
                nc.tensor.transpose(
                    pt[m][:, P * j : P * (j + 1)], prep[m // 2][:, P * c : P * (c + 1)], ident[:]
                )

        def weigh_h(m):
            hg[m] = h_pool.tile([P, 1024], BF16, name="hg", align_bytes=64)
            nc.vector.tensor_tensor(
                out=hg[m][:].rearrange("p (c i t) -> p c i t", i=4, t=4),
                in0=h1[m][:].rearrange("p c t i -> p c i t"),
                in1=pt[m][:].rearrange("p (c i) -> p c i", i=4).unsqueeze(3).to_broadcast([P, 64, 4, 4]),
                op=OP.mult,
            )

        def quant_h(m):
            hq[m] = (
                hq_pool.tile([P, 256], U32, name="hq_c", align_bytes=64),
                hq_pool.tile([P, 256], U8, name="hq_s", align_bytes=64),
            )
            nc.vector.quantize_mx(out=hq[m][0][:].bitcast(FP8X4), scales=hq[m][1][:], in_=hg[m][:])

        def mm2(i, e):
            m, j = i // 2, i % 2
            o_bank[i, e] = o_psum.tile([P, 512], F32, name="ob")
            nc.tensor.matmul_mx(
                out=o_bank[i, e][:],
                lhsT=hq[m][0][:, P * j : P * (j + 1)].bitcast(FP8X4),
                lhsT_scale=hq[m][1][:, P * j : P * (j + 1)],
                rhs=w2_c[:, 512 * e : 512 * (e + 1)].bitcast(FP8X4),
                rhs_scale=w2_s[:, 512 * e : 512 * (e + 1)],
                start=True,
                stop=True,
            )

        def leave_o(copy, i, e):
            if e == 0:
                o_sb[i] = o_pool.tile([P, E], F32, name="osb")
            copy(out=o_sb[i][:, 512 * e : 512 * (e + 1)], in_=o_bank[i, e][:])
            if e == 1:
                nc.sync.dma_start(out=out_v[:, i, :], in_=o_sb[i][:])

        for k in range(TILES + 10):
            if k < TILES:
                widen(k, 2 if k == 0 else 1)
            if k in (2, 3):
                w1_interleave(nc.vector.tensor_copy, 1, 2 * (k - 2))
                w1_interleave(nc.vector.tensor_copy, 1, 2 * (k - 2) + 1)
            if k % 2 == 1:
                m = (k - 3) // 2
                if 0 <= m < PAIRS:
                    quant_x(m)
                if k == 3:
                    w1_quantize(0)
                    w1_quantize(1)
                if k % 4 == 3 and (k - 3) // 4 < 8:
                    spread_p((k - 3) // 4)
                m = (k - 7) // 2
                if 0 <= m < PAIRS:
                    quant_h(m)
                if k == 7:
                    w2_quantize(0, 512)
            else:
                if k == 8:
                    w2_quantize(512, 1024)
                m = k // 2 - 3
                if 0 <= m < PAIRS:
                    weigh_h(m)
            if 0 <= k - 8 < TILES:
                mm2(k - 8, 0)
                mm2(k - 8, 1)
            m = (k - 4) // 2
            if 0 <= m < PAIRS:
                mm1(m, k % 2)
            if 0 <= k - 1 < TILES:
                turn_x(k - 1)
            if k % 2 == 1 and 0 <= (k - 5) // 2 < PAIRS:
                turn_p((k - 5) // 2)
            if k in (1, 2):
                w1_interleave(nc.scalar.copy, 0, 2 * (k - 1))
                w1_interleave(nc.scalar.copy, 0, 2 * (k - 1) + 1)
            if 0 <= k - 8 < TILES:
                leave_o(nc.scalar.copy, k - 8, 0)
            if 0 <= m < PAIRS:
                leave_h(m, k % 2)
            if 0 <= k - 1 < TILES:
                leave_x(k - 1)
            if 4 <= k < 8:
                w2_interleave(nc.scalar.copy, 256 * (k - 4), 256 * (k - 3))
            if 0 <= k - 8 < TILES:
                late = k >= TILES
                leave_o(nc.vector.tensor_copy if late else nc.scalar.copy, k - 8, 1)
